import numpy as np
import ml_dtypes

BF16 = ml_dtypes.bfloat16


def bf(x):
    return np.asarray(x, np.float32).astype(BF16)


def f32(x):
    return np.asarray(x, np.float32)


def f64(x):
    return np.asarray(x).astype(np.float64)


def striped(idx):
    return np.tile(idx.reshape(-1, 16).T, (8, 1))


C, FF, S, N, T, P = 256, 1024, 2048, 1024, 128, 8
EPS = 1e-6


def setup_inputs():
    ctx = 0.8 * np.random.standard_normal((C, N)) + 0.6 * np.repeat(np.random.standard_normal((C, P)), T, axis=1)
    return {"ctx": f32(ctx), "gain": f32(1.0 + 0.1 * np.random.standard_normal((C, 1))), "shift": f32(0.1 * np.random.standard_normal((C, 1))), "w1": bf(np.random.standard_normal((C, FF)) / np.sqrt(C)), "b1": f32(0.1 * np.random.standard_normal((FF, 1))), "w2": bf(np.random.standard_normal((FF, C)) * np.sqrt(2.0 / FF)), "b2": f32(0.1 * np.random.standard_normal((C, 1))), "base": f32(np.random.standard_normal((C, S))), "offs": striped(np.random.permutation(S)[:N])}


def reference(ctx, gain, shift, w1, b1, w2, b2, base, offs):
    idx = offs[:16].T.reshape(-1)
    c = f64(ctx)
    feat = c.reshape(C, P, T).mean(axis=2)
    x = c + np.repeat(feat, T, axis=1)
    mu = x.mean(axis=0, keepdims=True)
    var = ((x - mu) ** 2).mean(axis=0, keepdims=True)
    z = (x - mu) / np.sqrt(var + EPS) * f64(gain) + f64(shift)
    h = np.maximum(f64(w1).T @ z + f64(b1), 0.0)
    y = f64(w2).T @ h + f64(b2)
    out = f64(base).copy()
    out[:, idx] = y + x
    return out

@@ -1,0 +1,141 @@
+import concourse.mybir as mybir
+from concourse.masks import make_identity
+
+F32, BF16, U16 = mybir.dt.float32, mybir.dt.bfloat16, mybir.dt.uint16
+ALU = mybir.AluOpType
+FUNC = mybir.ActivationFunctionType
+
+P = 128
+C, FF, S, N, T = 256, 1024, 2048, 1024, 128
+EPS = 1e-6
+CB = C // P
+FB = FF // P
+TW = 256
+G = TW // T
+CHUNKS = N // TW
+BANK = 512
+HALVES = N // BANK
+
+GAIN, SHIFT, B2, B1 = 0, CB, 2 * CB, 3 * CB
+VECTOR_COLUMNS = 3 * CB + FB
+
+FLOPS = 2 * C * FF * N * 2
+
+
+def tile_emencoder_kernel(tc, ctx, gain, shift, w1, b1, w2, b2, base, offs, out):
+    nc = tc.nc
+    with (
+        tc.tile_pool(name="held", bufs=1) as held,
+        tc.tile_pool(name="work", bufs=2) as work,
+        tc.psum_pool(name="stat_psum", bufs=2) as stat_psum,
+        tc.psum_pool(name="h_psum", bufs=4) as h_psum,
+        tc.psum_pool(name="y_psum", bufs=2) as y_psum,
+    ):
+        ctx_blocks = ctx.rearrange("(b p) n -> p b n", p=P)
+        ctx_sb = held.tile([P, CB, N], F32, name="ctx_sb")
+        for c in range(CHUNKS):
+            nc.sync.dma_start(ctx_sb[:, :, c * TW : (c + 1) * TW], ctx_blocks[:, :, c * TW : (c + 1) * TW])
+        offsets = held.tile([P, N // 16], U16, name="offsets")
+        nc.sync.dma_start(offsets[:], offs)
+
+        vector_rows = held.tile([P, P], F32, name="vector_rows")
+        nc.gpsimd.memset(vector_rows[:], 0.0)
+        for first_row, vector in ((GAIN, gain), (SHIFT, shift), (B2, b2), (B1, b1)):
+            rows = vector.shape[0] // P
+            nc.scalar.dma_start(vector_rows[first_row : first_row + rows, :], vector.rearrange("(r p) o -> r (p o)", p=P))
+        w1_sb = held.tile([P, CB, FF], BF16, name="w1_sb")
+        nc.scalar.dma_start(w1_sb[:], w1.rearrange("(k p) f -> p k f", p=P))
+        w2_sb = held.tile([P, FB, C], BF16, name="w2_sb")
+        nc.scalar.dma_start(w2_sb[:], w2.rearrange("(f p) c -> p f c", p=P))
+        windows = [held.tile([P, S], F32, name=f"window{b}") for b in range(CB)]
+        for b in range(CB):
+            nc.gpsimd.dma_start(windows[b][:], base[b * P : (b + 1) * P, :])
+
+        identity = held.tile([P, P], F32, name="identity")
+        make_identity(nc, identity[:])
+        mean_weights = held.tile([P, P], F32, name="mean_weights")
+        nc.vector.memset(mean_weights[:], 1.0 / C)
+        eps = held.tile([P, 1], F32, name="eps")
+        nc.vector.memset(eps[:], EPS)
+
+        vector_columns = stat_psum.tile([P, P], F32, name="vector_columns", tag="stat")
+        nc.tensor.transpose(vector_columns[:], vector_rows[:], identity[:])
+        per_partition = held.tile([P, VECTOR_COLUMNS], F32, name="per_partition")
+        nc.vector.tensor_copy(per_partition[:], vector_columns[:, 0:VECTOR_COLUMNS])
+
+        def column(first, block):
+            return per_partition[:, first + block : first + block + 1]
+
+        x = held.tile([P, CB, N], F32, name="x")
+        h = held.tile([P, FB, N], BF16, name="h")
+        y = [held.tile([P, N], F32, name=f"y{b}") for b in range(CB)]
+
+        def normalize(c):
+            cols = slice(c * TW, (c + 1) * TW)
+            by_paragraph = "p b (g t) -> p b g t"
+            paragraph_sum = work.tile([P, CB, G], F32, name="paragraph_sum")
+            nc.vector.reduce_sum(paragraph_sum[:], ctx_sb[:, :, cols].rearrange(by_paragraph, t=T), axis=mybir.AxisListType.X)
+            nc.vector.scalar_tensor_tensor(
+                x[:, :, cols].rearrange(by_paragraph, t=T),
+                paragraph_sum[:].unsqueeze(3).to_broadcast([P, CB, G, T]),
+                1.0 / T,
+                ctx_sb[:, :, cols].rearrange(by_paragraph, t=T),
+                ALU.mult,
+                ALU.add,
+            )
+            x_blocks = work.tile([P, TW], F32, name="x_blocks")
+            nc.vector.tensor_tensor(x_blocks[:], x[:, 0, cols], x[:, 1, cols], ALU.add)
+            mu = stat_psum.tile([P, TW], F32, name="mu", tag="stat")
+            nc.tensor.matmul(mu[:], mean_weights[:], x_blocks[:], start=True, stop=True)
+            centred = work.tile([P, CB, TW], F32, name="centred")
+            nc.vector.tensor_tensor(centred[:], x[:, :, cols], mu[:].unsqueeze(1).to_broadcast([P, CB, TW]), ALU.subtract)
+            squares = work.tile([P, CB, TW], F32, name="squares")
+            nc.scalar.activation(squares[:], centred[:], FUNC.Square)
+            square_blocks = work.tile([P, TW], F32, name="square_blocks")
+            nc.vector.tensor_tensor(square_blocks[:], squares[:, 0, :], squares[:, 1, :], ALU.add)
+            var = stat_psum.tile([P, TW], F32, name="var", tag="stat")
+            nc.tensor.matmul(var[:], mean_weights[:], square_blocks[:], start=True, stop=True)
+            rstd = work.tile([P, TW], F32, name="rstd")
+            nc.scalar.activation(rstd[:], var[:], FUNC.Abs_reciprocal_sqrt, bias=eps[:])
+            scaled = work.tile([P, CB, TW], F32, name="scaled")
+            nc.vector.tensor_tensor(scaled[:], centred[:], rstd[:].unsqueeze(1).to_broadcast([P, CB, TW]), ALU.mult)
+            z = work.tile([P, CB, TW], BF16, name="z")
+            for b in range(CB):
+                nc.scalar.activation(z[:, b, :], scaled[:, b, :], FUNC.Identity, bias=column(SHIFT, b), scale=column(GAIN, b))
+            return z
+
+        def hidden(c, z):
+            cols = slice(c * TW, (c + 1) * TW)
+            for f in range(FB):
+                h_ps = h_psum.tile([P, TW], F32, name="h_ps")
+                for k in range(CB):
+                    nc.tensor.matmul(h_ps[:], w1_sb[:, k, f * P : (f + 1) * P], z[:, k, :], start=(k == 0), stop=(k == CB - 1))
+                if f % 4 == 3:
+                    nc.vector.tensor_scalar(h[:, f, cols], h_ps[:], column(B1, f), 0.0, ALU.add, ALU.max)
+                else:
+                    nc.scalar.activation(h[:, f, cols], h_ps[:], FUNC.Relu, bias=column(B1, f))
+
+        def project(b, half):
+            cols = slice(half * BANK, (half + 1) * BANK)
+            y_ps = y_psum.tile([P, BANK], F32, name="y_ps")
+            for f in range(FB):
+                nc.tensor.matmul(y_ps[:], w2_sb[:, f, b * P : (b + 1) * P], h[:, f, cols], start=(f == 0), stop=(f == FB - 1))
+            nc.scalar.activation(y[b][:, cols], y_ps[:], FUNC.Identity, bias=column(B2, b))
+
+        def place(b):
+            nc.vector.tensor_tensor(windows[b][:].indirect(offsets[:]), y[b][:], x[:, b, :], ALU.add)
+            nc.sync.dma_start(out[b * P : (b + 1) * P, 0 : S // 2], windows[b][:, 0 : S // 2])
+            nc.scalar.dma_start(out[b * P : (b + 1) * P, S // 2 : S], windows[b][:, S // 2 : S])
+
+        z_next = normalize(0)
+        for c in range(CHUNKS):
+            z_now = z_next
+            if c + 1 < CHUNKS:
+                z_next = normalize(c + 1)
+            hidden(c, z_now)
+            if (c + 1) * TW % BANK == 0:
+                project(0, (c + 1) * TW // BANK - 1)
+        place(0)
+        for half in range(HALVES):
+            project(1, half)
+        place(1)

@@ -26,30 +26,30 @@ def tile_emencoder_kernel(tc, ctx, gain, shift, w1, b1, w2, b2, base, offs, out)
     nc = tc.nc
     with (
         tc.tile_pool(name="held", bufs=1) as held,
-        tc.tile_pool(name="work", bufs=2) as work,
-        tc.psum_pool(name="stat_psum", bufs=2) as stat_psum,
-        tc.psum_pool(name="h_psum", bufs=4) as h_psum,
+        tc.tile_pool(name="work", bufs=CHUNKS) as work,
+        tc.psum_pool(name="stat_psum", bufs=3) as stat_psum,
+        tc.psum_pool(name="h_psum", bufs=3) as h_psum,
         tc.psum_pool(name="y_psum", bufs=2) as y_psum,
     ):
         ctx_blocks = ctx.rearrange("(b p) n -> p b n", p=P)
-        ctx_sb = held.tile([P, CB, N], F32, name="ctx_sb")
+        ctx_sb = held.tile([P, CHUNKS, CB, TW], F32, name="ctx_sb")
         for c in range(CHUNKS):
-            nc.sync.dma_start(ctx_sb[:, :, c * TW : (c + 1) * TW], ctx_blocks[:, :, c * TW : (c + 1) * TW])
+            nc.sync.dma_start(ctx_sb[:, c], ctx_blocks[:, :, c * TW : (c + 1) * TW])
+        w1_sb = held.tile([P, CB, FF], BF16, name="w1_sb")
+        nc.sync.dma_start(w1_sb[:], w1.rearrange("(k p) f -> p k f", p=P))
         offsets = held.tile([P, N // 16], U16, name="offsets")
         nc.sync.dma_start(offsets[:], offs)
+        w2_sb = held.tile([P, FB, C], BF16, name="w2_sb")
+        nc.sync.dma_start(w2_sb[:], w2.rearrange("(f p) c -> p f c", p=P))
+        windows = [held.tile([P, S], F32, name=f"window{b}") for b in range(CB)]
+        for b in range(CB):
+            nc.sync.dma_start(windows[b][:], base[b * P : (b + 1) * P, :])
 
         vector_rows = held.tile([P, P], F32, name="vector_rows")
         nc.gpsimd.memset(vector_rows[:], 0.0)
         for first_row, vector in ((GAIN, gain), (SHIFT, shift), (B2, b2), (B1, b1)):
             rows = vector.shape[0] // P
             nc.scalar.dma_start(vector_rows[first_row : first_row + rows, :], vector.rearrange("(r p) o -> r (p o)", p=P))
-        w1_sb = held.tile([P, CB, FF], BF16, name="w1_sb")
-        nc.scalar.dma_start(w1_sb[:], w1.rearrange("(k p) f -> p k f", p=P))
-        w2_sb = held.tile([P, FB, C], BF16, name="w2_sb")
-        nc.scalar.dma_start(w2_sb[:], w2.rearrange("(f p) c -> p f c", p=P))
-        windows = [held.tile([P, S], F32, name=f"window{b}") for b in range(CB)]
-        for b in range(CB):
-            nc.gpsimd.dma_start(windows[b][:], base[b * P : (b + 1) * P, :])
 
         identity = held.tile([P, P], F32, name="identity")
         make_identity(nc, identity[:])
@@ -58,7 +58,7 @@ def tile_emencoder_kernel(tc, ctx, gain, shift, w1, b1, w2, b2, base, offs, out)
         eps = held.tile([P, 1], F32, name="eps")
         nc.vector.memset(eps[:], EPS)
 
-        vector_columns = stat_psum.tile([P, P], F32, name="vector_columns", tag="stat")
+        vector_columns = y_psum.tile([P, P], F32, name="vector_columns", tag="y_ps")
         nc.tensor.transpose(vector_columns[:], vector_rows[:], identity[:])
         per_partition = held.tile([P, VECTOR_COLUMNS], F32, name="per_partition")
         nc.vector.tensor_copy(per_partition[:], vector_columns[:, 0:VECTOR_COLUMNS])
@@ -66,41 +66,42 @@ def tile_emencoder_kernel(tc, ctx, gain, shift, w1, b1, w2, b2, base, offs, out)
         def column(first, block):
             return per_partition[:, first + block : first + block + 1]
 
-        x = held.tile([P, CB, N], F32, name="x")
+        x = [held.tile([P, N], F32, name=f"x{b}") for b in range(CB)]
         h = held.tile([P, FB, N], BF16, name="h")
         y = [held.tile([P, N], F32, name=f"y{b}") for b in range(CB)]
 
         def normalize(c):
             cols = slice(c * TW, (c + 1) * TW)
-            by_paragraph = "p b (g t) -> p b g t"
             paragraph_sum = work.tile([P, CB, G], F32, name="paragraph_sum")
-            nc.vector.reduce_sum(paragraph_sum[:], ctx_sb[:, :, cols].rearrange(by_paragraph, t=T), axis=mybir.AxisListType.X)
-            nc.vector.scalar_tensor_tensor(
-                x[:, :, cols].rearrange(by_paragraph, t=T),
-                paragraph_sum[:].unsqueeze(3).to_broadcast([P, CB, G, T]),
-                1.0 / T,
-                ctx_sb[:, :, cols].rearrange(by_paragraph, t=T),
-                ALU.mult,
-                ALU.add,
-            )
+            nc.vector.reduce_sum(paragraph_sum[:], ctx_sb[:, c].rearrange("p b (g t) -> p b g t", t=T), axis=mybir.AxisListType.X)
+            for b in range(CB):
+                nc.vector.scalar_tensor_tensor(
+                    x[b][:, cols].rearrange("p (g t) -> p g t", t=T),
+                    paragraph_sum[:, b, :].unsqueeze(2).to_broadcast([P, G, T]),
+                    1.0 / T,
+                    ctx_sb[:, c, b, :].rearrange("p (g t) -> p g t", t=T),
+                    ALU.mult,
+                    ALU.add,
+                )
             x_blocks = work.tile([P, TW], F32, name="x_blocks")
-            nc.vector.tensor_tensor(x_blocks[:], x[:, 0, cols], x[:, 1, cols], ALU.add)
-            mu = stat_psum.tile([P, TW], F32, name="mu", tag="stat")
-            nc.tensor.matmul(mu[:], mean_weights[:], x_blocks[:], start=True, stop=True)
+            nc.vector.tensor_tensor(x_blocks[:], x[0][:, cols], x[1][:, cols], ALU.add)
+            stats = stat_psum.tile([P, 2, TW], F32, name="stats")
+            mu, var = stats[:, 0, :], stats[:, 1, :]
+            nc.tensor.matmul(mu, mean_weights[:], x_blocks[:], start=True, stop=True)
             centred = work.tile([P, CB, TW], F32, name="centred")
-            nc.vector.tensor_tensor(centred[:], x[:, :, cols], mu[:].unsqueeze(1).to_broadcast([P, CB, TW]), ALU.subtract)
             squares = work.tile([P, CB, TW], F32, name="squares")
-            nc.scalar.activation(squares[:], centred[:], FUNC.Square)
+            for b in range(CB):
+                nc.vector.tensor_tensor(centred[:, b, :], x[b][:, cols], mu, ALU.subtract)
+                nc.scalar.activation(squares[:, b, :], centred[:, b, :], FUNC.Square)
             square_blocks = work.tile([P, TW], F32, name="square_blocks")
             nc.vector.tensor_tensor(square_blocks[:], squares[:, 0, :], squares[:, 1, :], ALU.add)
-            var = stat_psum.tile([P, TW], F32, name="var", tag="stat")
-            nc.tensor.matmul(var[:], mean_weights[:], square_blocks[:], start=True, stop=True)
+            nc.tensor.matmul(var, mean_weights[:], square_blocks[:], start=True, stop=True)
             rstd = work.tile([P, TW], F32, name="rstd")
-            nc.scalar.activation(rstd[:], var[:], FUNC.Abs_reciprocal_sqrt, bias=eps[:])
+            nc.scalar.activation(rstd[:], var, FUNC.Abs_reciprocal_sqrt, bias=eps[:])
             scaled = work.tile([P, CB, TW], F32, name="scaled")
-            nc.vector.tensor_tensor(scaled[:], centred[:], rstd[:].unsqueeze(1).to_broadcast([P, CB, TW]), ALU.mult)
             z = work.tile([P, CB, TW], BF16, name="z")
             for b in range(CB):
+                nc.vector.tensor_tensor(scaled[:, b, :], centred[:, b, :], rstd[:], ALU.mult)
                 nc.scalar.activation(z[:, b, :], scaled[:, b, :], FUNC.Identity, bias=column(SHIFT, b), scale=column(GAIN, b))
             return z
 
@@ -123,16 +124,13 @@ def tile_emencoder_kernel(tc, ctx, gain, shift, w1, b1, w2, b2, base, offs, out)
             nc.scalar.activation(y[b][:, cols], y_ps[:], FUNC.Identity, bias=column(B2, b))
 
         def place(b):
-            nc.vector.tensor_tensor(windows[b][:].indirect(offsets[:]), y[b][:], x[:, b, :], ALU.add)
+            nc.vector.tensor_tensor(windows[b][:].indirect(offsets[:]), y[b][:], x[b][:], ALU.add)
             nc.sync.dma_start(out[b * P : (b + 1) * P, 0 : S // 2], windows[b][:, 0 : S // 2])
             nc.scalar.dma_start(out[b * P : (b + 1) * P, S // 2 : S], windows[b][:, S // 2 : S])
 
-        z_next = normalize(0)
+        z_of_chunk = [normalize(c) for c in range(CHUNKS)]
         for c in range(CHUNKS):
-            z_now = z_next
-            if c + 1 < CHUNKS:
-                z_next = normalize(c + 1)
-            hidden(c, z_now)
+            hidden(c, z_of_chunk[c])
             if (c + 1) * TW % BANK == 0:
                 project(0, (c + 1) * TW // BANK - 1)
         place(0)

@@ -15,6 +15,7 @@ G = TW // T
 CHUNKS = N // TW
 BANK = 512
 HALVES = N // BANK
+WARM_UP_MATMULS = 12
 
 GAIN, SHIFT, B2, B1 = 0, CB, 2 * CB, 3 * CB
 VECTOR_COLUMNS = 3 * CB + FB
@@ -27,9 +28,8 @@ def tile_emencoder_kernel(tc, ctx, gain, shift, w1, b1, w2, b2, base, offs, out)
     with (
         tc.tile_pool(name="held", bufs=1) as held,
         tc.tile_pool(name="work", bufs=CHUNKS) as work,
-        tc.psum_pool(name="stat_psum", bufs=3) as stat_psum,
-        tc.psum_pool(name="h_psum", bufs=3) as h_psum,
-        tc.psum_pool(name="y_psum", bufs=2) as y_psum,
+        tc.psum_pool(name="h_psum", bufs=4) as h_psum,
+        tc.psum_pool(name="other_psum", bufs=4) as other_psum,
     ):
         ctx_blocks = ctx.rearrange("(b p) n -> p b n", p=P)
         ctx_sb = held.tile([P, CHUNKS, CB, TW], F32, name="ctx_sb")
@@ -51,6 +51,11 @@ def tile_emencoder_kernel(tc, ctx, gain, shift, w1, b1, w2, b2, base, offs, out)
             rows = vector.shape[0] // P
             nc.scalar.dma_start(vector_rows[first_row : first_row + rows, :], vector.rearrange("(r p) o -> r (p o)", p=P))
 
+        zeros = held.tile([P, BANK], BF16, name="zeros")
+        nc.vector.memset(zeros[:], 0.0)
+        unused_ps = h_psum.tile([P, BANK], F32, name="unused_ps", tag="h_ps")
+        for i in range(WARM_UP_MATMULS):
+            nc.tensor.matmul(unused_ps[:], zeros[:, 0:P], zeros[:], start=True, stop=True)
         identity = held.tile([P, P], F32, name="identity")
         make_identity(nc, identity[:])
         mean_weights = held.tile([P, P], F32, name="mean_weights")
@@ -58,7 +63,7 @@ def tile_emencoder_kernel(tc, ctx, gain, shift, w1, b1, w2, b2, base, offs, out)
         eps = held.tile([P, 1], F32, name="eps")
         nc.vector.memset(eps[:], EPS)
 
-        vector_columns = y_psum.tile([P, P], F32, name="vector_columns", tag="y_ps")
+        vector_columns = other_psum.tile([P, P], F32, name="vector_columns", tag="bank")
         nc.tensor.transpose(vector_columns[:], vector_rows[:], identity[:])
         per_partition = held.tile([P, VECTOR_COLUMNS], F32, name="per_partition")
         nc.vector.tensor_copy(per_partition[:], vector_columns[:, 0:VECTOR_COLUMNS])
@@ -67,6 +72,7 @@ def tile_emencoder_kernel(tc, ctx, gain, shift, w1, b1, w2, b2, base, offs, out)
             return per_partition[:, first + block : first + block + 1]
 
         x = [held.tile([P, N], F32, name=f"x{b}") for b in range(CB)]
+        z = [held.tile([P, CB, BANK], BF16, name=f"z{half}") for half in range(HALVES)]
         h = held.tile([P, FB, N], BF16, name="h")
         y = [held.tile([P, N], F32, name=f"y{b}") for b in range(CB)]
 
@@ -85,7 +91,7 @@ def tile_emencoder_kernel(tc, ctx, gain, shift, w1, b1, w2, b2, base, offs, out)
                 )
             x_blocks = work.tile([P, TW], F32, name="x_blocks")
             nc.vector.tensor_tensor(x_blocks[:], x[0][:, cols], x[1][:, cols], ALU.add)
-            stats = stat_psum.tile([P, 2, TW], F32, name="stats")
+            stats = other_psum.tile([P, 2, TW], F32, name="stats", tag="bank")
             mu, var = stats[:, 0, :], stats[:, 1, :]
             nc.tensor.matmul(mu, mean_weights[:], x_blocks[:], start=True, stop=True)
             centred = work.tile([P, CB, TW], F32, name="centred")
@@ -99,18 +105,19 @@ def tile_emencoder_kernel(tc, ctx, gain, shift, w1, b1, w2, b2, base, offs, out)
             rstd = work.tile([P, TW], F32, name="rstd")
             nc.scalar.activation(rstd[:], var, FUNC.Abs_reciprocal_sqrt, bias=eps[:])
             scaled = work.tile([P, CB, TW], F32, name="scaled")
-            z = work.tile([P, CB, TW], BF16, name="z")
+            half, first = c * TW // BANK, c * TW % BANK
             for b in range(CB):
                 nc.vector.tensor_tensor(scaled[:, b, :], centred[:, b, :], rstd[:], ALU.mult)
-                nc.scalar.activation(z[:, b, :], scaled[:, b, :], FUNC.Identity, bias=column(SHIFT, b), scale=column(GAIN, b))
-            return z
+                nc.scalar.activation(
+                    z[half][:, b, first : first + TW], scaled[:, b, :], FUNC.Identity, bias=column(SHIFT, b), scale=column(GAIN, b)
+                )
 
-        def hidden(c, z):
-            cols = slice(c * TW, (c + 1) * TW)
+        def hidden(half):
+            cols = slice(half * BANK, (half + 1) * BANK)
             for f in range(FB):
-                h_ps = h_psum.tile([P, TW], F32, name="h_ps")
+                h_ps = h_psum.tile([P, BANK], F32, name="h_ps")
                 for k in range(CB):
-                    nc.tensor.matmul(h_ps[:], w1_sb[:, k, f * P : (f + 1) * P], z[:, k, :], start=(k == 0), stop=(k == CB - 1))
+                    nc.tensor.matmul(h_ps[:], w1_sb[:, k, f * P : (f + 1) * P], z[half][:, k, :], start=(k == 0), stop=(k == CB - 1))
                 if f % 4 == 3:
                     nc.vector.tensor_scalar(h[:, f, cols], h_ps[:], column(B1, f), 0.0, ALU.add, ALU.max)
                 else:
@@ -118,7 +125,7 @@ def tile_emencoder_kernel(tc, ctx, gain, shift, w1, b1, w2, b2, base, offs, out)
 
         def project(b, half):
             cols = slice(half * BANK, (half + 1) * BANK)
-            y_ps = y_psum.tile([P, BANK], F32, name="y_ps")
+            y_ps = other_psum.tile([P, BANK], F32, name="y_ps", tag="bank")
             for f in range(FB):
                 nc.tensor.matmul(y_ps[:], w2_sb[:, f, b * P : (b + 1) * P], h[:, f, cols], start=(f == 0), stop=(f == FB - 1))
             nc.scalar.activation(y[b][:, cols], y_ps[:], FUNC.Identity, bias=column(B2, b))
@@ -128,11 +135,11 @@ def tile_emencoder_kernel(tc, ctx, gain, shift, w1, b1, w2, b2, base, offs, out)
             nc.sync.dma_start(out[b * P : (b + 1) * P, 0 : S // 2], windows[b][:, 0 : S // 2])
             nc.scalar.dma_start(out[b * P : (b + 1) * P, S // 2 : S], windows[b][:, S // 2 : S])
 
-        z_of_chunk = [normalize(c) for c in range(CHUNKS)]
         for c in range(CHUNKS):
-            hidden(c, z_of_chunk[c])
-            if (c + 1) * TW % BANK == 0:
-                project(0, (c + 1) * TW // BANK - 1)
+            normalize(c)
+        for half in range(HALVES):
+            hidden(half)
+            project(0, half)
         place(0)
         for half in range(HALVES):
             project(1, half)

@@ -28,8 +28,8 @@ def tile_emencoder_kernel(tc, ctx, gain, shift, w1, b1, w2, b2, base, offs, out)
     with (
         tc.tile_pool(name="held", bufs=1) as held,
         tc.tile_pool(name="work", bufs=CHUNKS) as work,
-        tc.psum_pool(name="h_psum", bufs=4) as h_psum,
-        tc.psum_pool(name="other_psum", bufs=4) as other_psum,
+        tc.psum_pool(name="bank_psum", bufs=6) as bank_psum,
+        tc.psum_pool(name="y_psum", bufs=1) as y_psum,
     ):
         ctx_blocks = ctx.rearrange("(b p) n -> p b n", p=P)
         ctx_sb = held.tile([P, CHUNKS, CB, TW], F32, name="ctx_sb")
@@ -53,7 +53,7 @@ def tile_emencoder_kernel(tc, ctx, gain, shift, w1, b1, w2, b2, base, offs, out)
 
         zeros = held.tile([P, BANK], BF16, name="zeros")
         nc.vector.memset(zeros[:], 0.0)
-        unused_ps = h_psum.tile([P, BANK], F32, name="unused_ps", tag="h_ps")
+        unused_ps = bank_psum.tile([P, BANK], F32, name="unused_ps", tag="bank")
         for i in range(WARM_UP_MATMULS):
             nc.tensor.matmul(unused_ps[:], zeros[:, 0:P], zeros[:], start=True, stop=True)
         identity = held.tile([P, P], F32, name="identity")
@@ -63,7 +63,7 @@ def tile_emencoder_kernel(tc, ctx, gain, shift, w1, b1, w2, b2, base, offs, out)
         eps = held.tile([P, 1], F32, name="eps")
         nc.vector.memset(eps[:], EPS)
 
-        vector_columns = other_psum.tile([P, P], F32, name="vector_columns", tag="bank")
+        vector_columns = bank_psum.tile([P, P], F32, name="vector_columns", tag="bank")
         nc.tensor.transpose(vector_columns[:], vector_rows[:], identity[:])
         per_partition = held.tile([P, VECTOR_COLUMNS], F32, name="per_partition")
         nc.vector.tensor_copy(per_partition[:], vector_columns[:, 0:VECTOR_COLUMNS])
@@ -90,8 +90,8 @@ def tile_emencoder_kernel(tc, ctx, gain, shift, w1, b1, w2, b2, base, offs, out)
                     ALU.add,
                 )
             x_blocks = work.tile([P, TW], F32, name="x_blocks")
-            nc.vector.tensor_tensor(x_blocks[:], x[0][:, cols], x[1][:, cols], ALU.add)
-            stats = other_psum.tile([P, 2, TW], F32, name="stats", tag="bank")
+            nc.gpsimd.tensor_tensor(x_blocks[:], x[0][:, cols], x[1][:, cols], ALU.add)
+            stats = bank_psum.tile([P, 2, TW], F32, name="stats", tag="bank")
             mu, var = stats[:, 0, :], stats[:, 1, :]
             nc.tensor.matmul(mu, mean_weights[:], x_blocks[:], start=True, stop=True)
             centred = work.tile([P, CB, TW], F32, name="centred")
@@ -100,7 +100,7 @@ def tile_emencoder_kernel(tc, ctx, gain, shift, w1, b1, w2, b2, base, offs, out)
                 nc.vector.tensor_tensor(centred[:, b, :], x[b][:, cols], mu, ALU.subtract)
                 nc.scalar.activation(squares[:, b, :], centred[:, b, :], FUNC.Square)
             square_blocks = work.tile([P, TW], F32, name="square_blocks")
-            nc.vector.tensor_tensor(square_blocks[:], squares[:, 0, :], squares[:, 1, :], ALU.add)
+            nc.gpsimd.tensor_tensor(square_blocks[:], squares[:, 0, :], squares[:, 1, :], ALU.add)
             nc.tensor.matmul(var, mean_weights[:], square_blocks[:], start=True, stop=True)
             rstd = work.tile([P, TW], F32, name="rstd")
             nc.scalar.activation(rstd[:], var, FUNC.Abs_reciprocal_sqrt, bias=eps[:])
@@ -115,7 +115,7 @@ def tile_emencoder_kernel(tc, ctx, gain, shift, w1, b1, w2, b2, base, offs, out)
         def hidden(half):
             cols = slice(half * BANK, (half + 1) * BANK)
             for f in range(FB):
-                h_ps = h_psum.tile([P, BANK], F32, name="h_ps")
+                h_ps = bank_psum.tile([P, BANK], F32, name="h_ps", tag="bank")
                 for k in range(CB):
                     nc.tensor.matmul(h_ps[:], w1_sb[:, k, f * P : (f + 1) * P], z[half][:, k, :], start=(k == 0), stop=(k == CB - 1))
                 if f % 4 == 3:
@@ -123,24 +123,22 @@ def tile_emencoder_kernel(tc, ctx, gain, shift, w1, b1, w2, b2, base, offs, out)
                 else:
                     nc.scalar.activation(h[:, f, cols], h_ps[:], FUNC.Relu, bias=column(B1, f))
 
-        def project(b, half):
+        def project(b, half, y_ps):
             cols = slice(half * BANK, (half + 1) * BANK)
-            y_ps = other_psum.tile([P, BANK], F32, name="y_ps", tag="bank")
             for f in range(FB):
-                nc.tensor.matmul(y_ps[:], w2_sb[:, f, b * P : (b + 1) * P], h[:, f, cols], start=(f == 0), stop=(f == FB - 1))
-            nc.scalar.activation(y[b][:, cols], y_ps[:], FUNC.Identity, bias=column(B2, b))
+                nc.tensor.matmul(y_ps[:, half, :], w2_sb[:, f, b * P : (b + 1) * P], h[:, f, cols], start=(f == 0), stop=(f == FB - 1))
+            nc.scalar.activation(y[b][:, cols], y_ps[:, half, :], FUNC.Identity, bias=column(B2, b))
 
         def place(b):
             nc.vector.tensor_tensor(windows[b][:].indirect(offsets[:]), y[b][:], x[b][:], ALU.add)
-            nc.sync.dma_start(out[b * P : (b + 1) * P, 0 : S // 2], windows[b][:, 0 : S // 2])
-            nc.scalar.dma_start(out[b * P : (b + 1) * P, S // 2 : S], windows[b][:, S // 2 : S])
+            nc.sync.dma_start(out[b * P : (b + 1) * P, :], windows[b][:])
 
         for c in range(CHUNKS):
             normalize(c)
-        for half in range(HALVES):
-            hidden(half)
-            project(0, half)
-        place(0)
-        for half in range(HALVES):
-            project(1, half)
-        place(1)
+        for b in range(CB):
+            y_ps = y_psum.tile([P, HALVES, BANK], F32, name="y_ps")
+            for half in range(HALVES):
+                if b == 0:
+                    hidden(half)
+                project(b, half, y_ps)
+            place(b)

@@ -90,7 +90,7 @@ def tile_emencoder_kernel(tc, ctx, gain, shift, w1, b1, w2, b2, base, offs, out)
                     ALU.add,
                 )
             x_blocks = work.tile([P, TW], F32, name="x_blocks")
-            nc.gpsimd.tensor_tensor(x_blocks[:], x[0][:, cols], x[1][:, cols], ALU.add)
+            nc.vector.tensor_tensor(x_blocks[:], x[0][:, cols], x[1][:, cols], ALU.add)
             stats = bank_psum.tile([P, 2, TW], F32, name="stats", tag="bank")
             mu, var = stats[:, 0, :], stats[:, 1, :]
             nc.tensor.matmul(mu, mean_weights[:], x_blocks[:], start=True, stop=True)
@@ -100,7 +100,7 @@ def tile_emencoder_kernel(tc, ctx, gain, shift, w1, b1, w2, b2, base, offs, out)
                 nc.vector.tensor_tensor(centred[:, b, :], x[b][:, cols], mu, ALU.subtract)
                 nc.scalar.activation(squares[:, b, :], centred[:, b, :], FUNC.Square)
             square_blocks = work.tile([P, TW], F32, name="square_blocks")
-            nc.gpsimd.tensor_tensor(square_blocks[:], squares[:, 0, :], squares[:, 1, :], ALU.add)
+            nc.vector.tensor_tensor(square_blocks[:], squares[:, 0, :], squares[:, 1, :], ALU.add)
             nc.tensor.matmul(var, mean_weights[:], square_blocks[:], start=True, stop=True)
             rstd = work.tile([P, TW], F32, name="rstd")
             nc.scalar.activation(rstd[:], var, FUNC.Abs_reciprocal_sqrt, bias=eps[:])

@@ -118,7 +118,7 @@ def tile_emencoder_kernel(tc, ctx, gain, shift, w1, b1, w2, b2, base, offs, out)
                 h_ps = bank_psum.tile([P, BANK], F32, name="h_ps", tag="bank")
                 for k in range(CB):
                     nc.tensor.matmul(h_ps[:], w1_sb[:, k, f * P : (f + 1) * P], z[half][:, k, :], start=(k == 0), stop=(k == CB - 1))
-                if f % 4 == 3:
+                if f % 2 == 1:
                     nc.vector.tensor_scalar(h[:, f, cols], h_ps[:], column(B1, f), 0.0, ALU.add, ALU.max)
                 else:
                     nc.scalar.activation(h[:, f, cols], h_ps[:], FUNC.Relu, bias=column(B1, f))

@@ -28,7 +28,9 @@ def tile_emencoder_kernel(tc, ctx, gain, shift, w1, b1, w2, b2, base, offs, out)
     with (
         tc.tile_pool(name="held", bufs=1) as held,
         tc.tile_pool(name="work", bufs=CHUNKS) as work,
-        tc.psum_pool(name="bank_psum", bufs=6) as bank_psum,
+        tc.psum_pool(name="bank_psum", bufs=3) as bank_psum,
+        tc.psum_pool(name="turned_psum", bufs=2) as turned_psum,
+        tc.psum_pool(name="normed_psum", bufs=1) as normed_psum,
         tc.psum_pool(name="y_psum", bufs=1) as y_psum,
     ):
         ctx_blocks = ctx.rearrange("(b p) n -> p b n", p=P)
@@ -58,8 +60,6 @@ def tile_emencoder_kernel(tc, ctx, gain, shift, w1, b1, w2, b2, base, offs, out)
             nc.tensor.matmul(unused_ps[:], zeros[:, 0:P], zeros[:], start=True, stop=True)
         identity = held.tile([P, P], F32, name="identity")
         make_identity(nc, identity[:])
-        mean_weights = held.tile([P, P], F32, name="mean_weights")
-        nc.vector.memset(mean_weights[:], 1.0 / C)
         eps = held.tile([P, 1], F32, name="eps")
         nc.vector.memset(eps[:], EPS)
 
@@ -72,7 +72,7 @@ def tile_emencoder_kernel(tc, ctx, gain, shift, w1, b1, w2, b2, base, offs, out)
             return per_partition[:, first + block : first + block + 1]
 
         x = [held.tile([P, N], F32, name=f"x{b}") for b in range(CB)]
-        z = [held.tile([P, CB, BANK], BF16, name=f"z{half}") for half in range(HALVES)]
+        z = [held.tile([P, CB, TW], BF16, name=f"z{c}") for c in range(CHUNKS)]
         h = held.tile([P, FB, N], BF16, name="h")
         y = [held.tile([P, N], F32, name=f"y{b}") for b in range(CB)]
 
@@ -89,45 +89,50 @@ def tile_emencoder_kernel(tc, ctx, gain, shift, w1, b1, w2, b2, base, offs, out)
                     ALU.mult,
                     ALU.add,
                 )
-            x_blocks = work.tile([P, TW], F32, name="x_blocks")
-            nc.vector.tensor_tensor(x_blocks[:], x[0][:, cols], x[1][:, cols], ALU.add)
-            stats = bank_psum.tile([P, 2, TW], F32, name="stats", tag="bank")
-            mu, var = stats[:, 0, :], stats[:, 1, :]
-            nc.tensor.matmul(mu, mean_weights[:], x_blocks[:], start=True, stop=True)
-            centred = work.tile([P, CB, TW], F32, name="centred")
-            squares = work.tile([P, CB, TW], F32, name="squares")
-            for b in range(CB):
-                nc.vector.tensor_tensor(centred[:, b, :], x[b][:, cols], mu, ALU.subtract)
-                nc.scalar.activation(squares[:, b, :], centred[:, b, :], FUNC.Square)
-            square_blocks = work.tile([P, TW], F32, name="square_blocks")
-            nc.vector.tensor_tensor(square_blocks[:], squares[:, 0, :], squares[:, 1, :], ALU.add)
-            nc.tensor.matmul(var, mean_weights[:], square_blocks[:], start=True, stop=True)
-            rstd = work.tile([P, TW], F32, name="rstd")
-            nc.scalar.activation(rstd[:], var, FUNC.Abs_reciprocal_sqrt, bias=eps[:])
-            scaled = work.tile([P, CB, TW], F32, name="scaled")
-            half, first = c * TW // BANK, c * TW % BANK
-            for b in range(CB):
-                nc.vector.tensor_tensor(scaled[:, b, :], centred[:, b, :], rstd[:], ALU.mult)
-                nc.scalar.activation(
-                    z[half][:, b, first : first + TW], scaled[:, b, :], FUNC.Identity, bias=column(SHIFT, b), scale=column(GAIN, b)
+            x_turned = turned_psum.tile([P, G, C], F32, name="x_turned")
+            for g in range(G):
+                first_token = c * TW + g * T
+                for b in range(CB):
+                    nc.tensor.transpose(x_turned[:, g, b * P : (b + 1) * P], x[b][:, first_token : first_token + T], identity[:])
+            partial = work.tile([P, G, 6], F32, name="partial")
+            mean_var = work.tile([P, G, 2], F32, name="mean_var")
+            for g in range(G):
+                nc.vector.bn_stats(partial[:, g, :], x_turned[:, g, :])
+                nc.vector.bn_aggr(mean_var[:, g, :], partial[:, g, :])
+            rstd = work.tile([P, G], F32, name="rstd")
+            nc.scalar.activation(rstd[:], mean_var[:, :, 1], FUNC.Abs_reciprocal_sqrt, bias=eps[:])
+            normed_turned = work.tile([P, G, C], F32, name="normed_turned")
+            for g in range(G):
+                nc.vector.tensor_scalar(
+                    normed_turned[:, g, :], x_turned[:, g, :], mean_var[:, g, 0:1], rstd[:, g : g + 1], ALU.subtract, ALU.mult
                 )
+            normed = normed_psum.tile([P, CB, TW], F32, name="normed")
+            for b in range(CB):
+                for g in range(G):
+                    nc.tensor.transpose(normed[:, b, g * T : (g + 1) * T], normed_turned[:, g, b * P : (b + 1) * P], identity[:])
+            for b in range(CB):
+                nc.scalar.activation(z[c][:, b, :], normed[:, b, :], FUNC.Identity, bias=column(SHIFT, b), scale=column(GAIN, b))
 
-        def hidden(half):
-            cols = slice(half * BANK, (half + 1) * BANK)
-            for f in range(FB):
-                h_ps = bank_psum.tile([P, BANK], F32, name="h_ps", tag="bank")
-                for k in range(CB):
-                    nc.tensor.matmul(h_ps[:], w1_sb[:, k, f * P : (f + 1) * P], z[half][:, k, :], start=(k == 0), stop=(k == CB - 1))
-                if f % 2 == 1:
-                    nc.vector.tensor_scalar(h[:, f, cols], h_ps[:], column(B1, f), 0.0, ALU.add, ALU.max)
-                else:
-                    nc.scalar.activation(h[:, f, cols], h_ps[:], FUNC.Relu, bias=column(B1, f))
+        def hidden(c):
+            cols = slice(c * TW, (c + 1) * TW)
+            for pair in range(FB // 2):
+                h_ps = bank_psum.tile([P, 2, TW], F32, name="h_ps", tag="bank")
+                for i in range(2):
+                    f = 2 * pair + i
+                    for k in range(CB):
+                        nc.tensor.matmul(h_ps[:, i, :], w1_sb[:, k, f * P : (f + 1) * P], z[c][:, k, :], start=(k == 0), stop=(k == CB - 1))
+                for i in range(2):
+                    f = 2 * pair + i
+                    if pair % 4 == 3:
+                        nc.vector.tensor_scalar(h[:, f, cols], h_ps[:, i, :], column(B1, f), 0.0, ALU.add, ALU.max)
+                    else:
+                        nc.scalar.activation(h[:, f, cols], h_ps[:, i, :], FUNC.Relu, bias=column(B1, f))
 
-        def project(b, half, y_ps):
-            cols = slice(half * BANK, (half + 1) * BANK)
+        def project(b, first, width, y_ps):
+            cols = slice(first, first + width)
             for f in range(FB):
-                nc.tensor.matmul(y_ps[:, half, :], w2_sb[:, f, b * P : (b + 1) * P], h[:, f, cols], start=(f == 0), stop=(f == FB - 1))
-            nc.scalar.activation(y[b][:, cols], y_ps[:, half, :], FUNC.Identity, bias=column(B2, b))
+                nc.tensor.matmul(y_ps[:, cols], w2_sb[:, f, b * P : (b + 1) * P], h[:, f, cols], start=(f == 0), stop=(f == FB - 1))
+            nc.scalar.activation(y[b][:, cols], y_ps[:, cols], FUNC.Identity, bias=column(B2, b))
 
         def place(b):
             nc.vector.tensor_tensor(windows[b][:].indirect(offsets[:]), y[b][:], x[b][:], ALU.add)
@@ -135,10 +140,12 @@ def tile_emencoder_kernel(tc, ctx, gain, shift, w1, b1, w2, b2, base, offs, out)
 
         for c in range(CHUNKS):
             normalize(c)
-        for b in range(CB):
-            y_ps = y_psum.tile([P, HALVES, BANK], F32, name="y_ps")
-            for half in range(HALVES):
-                if b == 0:
-                    hidden(half)
-                project(b, half, y_ps)
-            place(b)
+        y_ps = y_psum.tile([P, N], F32, name="y_ps")
+        for c in range(CHUNKS):
+            hidden(c)
+            project(0, c * TW, TW, y_ps)
+        place(0)
+        y_ps = y_psum.tile([P, N], F32, name="y_ps")
+        for half in range(HALVES):
+            project(1, half * BANK, BANK, y_ps)
+        place(1)

@@ -15,7 +15,7 @@ G = TW // T
 CHUNKS = N // TW
 BANK = 512
 HALVES = N // BANK
-WARM_UP_MATMULS = 12
+WARM_UP_MATMULS = 8
 
 GAIN, SHIFT, B2, B1 = 0, CB, 2 * CB, 3 * CB
 VECTOR_COLUMNS = 3 * CB + FB
@@ -53,11 +53,6 @@ def tile_emencoder_kernel(tc, ctx, gain, shift, w1, b1, w2, b2, base, offs, out)
             rows = vector.shape[0] // P
             nc.scalar.dma_start(vector_rows[first_row : first_row + rows, :], vector.rearrange("(r p) o -> r (p o)", p=P))
 
-        zeros = held.tile([P, BANK], BF16, name="zeros")
-        nc.vector.memset(zeros[:], 0.0)
-        unused_ps = bank_psum.tile([P, BANK], F32, name="unused_ps", tag="bank")
-        for i in range(WARM_UP_MATMULS):
-            nc.tensor.matmul(unused_ps[:], zeros[:, 0:P], zeros[:], start=True, stop=True)
         identity = held.tile([P, P], F32, name="identity")
         make_identity(nc, identity[:])
         eps = held.tile([P, 1], F32, name="eps")
@@ -140,6 +135,9 @@ def tile_emencoder_kernel(tc, ctx, gain, shift, w1, b1, w2, b2, base, offs, out)
 
         for c in range(CHUNKS):
             normalize(c)
+        unused_ps = bank_psum.tile([P, BANK], F32, name="unused_ps", tag="bank")
+        for i in range(WARM_UP_MATMULS):
+            nc.tensor.matmul(unused_ps[:], w1_sb[:, 0, 0:P], w1_sb[:, 0, 0:BANK], start=True, stop=True)
         y_ps = y_psum.tile([P, N], F32, name="y_ps")
         for c in range(CHUNKS):
             hidden(c)

@@ -35,8 +35,14 @@ def tile_emencoder_kernel(tc, ctx, gain, shift, w1, b1, w2, b2, base, offs, out)
     ):
         ctx_blocks = ctx.rearrange("(b p) n -> p b n", p=P)
         ctx_sb = held.tile([P, CHUNKS, CB, TW], F32, name="ctx_sb")
+        vector_rows = held.tile([P, P], F32, name="vector_rows")
+        nc.gpsimd.memset(vector_rows[:], 0.0)
         for c in range(CHUNKS):
             nc.sync.dma_start(ctx_sb[:, c], ctx_blocks[:, :, c * TW : (c + 1) * TW])
+            if c == 0:
+                for first_row, vector in ((GAIN, gain), (SHIFT, shift), (B2, b2), (B1, b1)):
+                    rows = vector.shape[0] // P
+                    nc.sync.dma_start(vector_rows[first_row : first_row + rows, :], vector.rearrange("(r p) o -> r (p o)", p=P))
         w1_sb = held.tile([P, CB, FF], BF16, name="w1_sb")
         nc.sync.dma_start(w1_sb[:], w1.rearrange("(k p) f -> p k f", p=P))
         offsets = held.tile([P, N // 16], U16, name="offsets")
@@ -47,16 +53,13 @@ def tile_emencoder_kernel(tc, ctx, gain, shift, w1, b1, w2, b2, base, offs, out)
         for b in range(CB):
             nc.sync.dma_start(windows[b][:], base[b * P : (b + 1) * P, :])
 
-        vector_rows = held.tile([P, P], F32, name="vector_rows")
-        nc.gpsimd.memset(vector_rows[:], 0.0)
-        for first_row, vector in ((GAIN, gain), (SHIFT, shift), (B2, b2), (B1, b1)):
-            rows = vector.shape[0] // P
-            nc.scalar.dma_start(vector_rows[first_row : first_row + rows, :], vector.rearrange("(r p) o -> r (p o)", p=P))
 
         identity = held.tile([P, P], F32, name="identity")
         make_identity(nc, identity[:])
         eps = held.tile([P, 1], F32, name="eps")
         nc.vector.memset(eps[:], EPS)
+        unused_rstd = held.tile([P, 1], F32, name="unused_rstd")
+        nc.scalar.activation(unused_rstd[:], eps[:], FUNC.Abs_reciprocal_sqrt, bias=eps[:])
 
         vector_columns = bank_psum.tile([P, P], F32, name="vector_columns", tag="bank")
         nc.tensor.transpose(vector_columns[:], vector_rows[:], identity[:])
@@ -73,16 +76,26 @@ def tile_emencoder_kernel(tc, ctx, gain, shift, w1, b1, w2, b2, base, offs, out)
 
         def normalize(c):
             cols = slice(c * TW, (c + 1) * TW)
-            paragraph_sum = work.tile([P, CB, G], F32, name="paragraph_sum")
-            nc.vector.reduce_sum(paragraph_sum[:], ctx_sb[:, c].rearrange("p b (g t) -> p b g t", t=T), axis=mybir.AxisListType.X)
-            for b in range(CB):
-                nc.vector.scalar_tensor_tensor(
-                    x[b][:, cols].rearrange("p (g t) -> p g t", t=T),
-                    paragraph_sum[:, b, :].unsqueeze(2).to_broadcast([P, G, T]),
-                    1.0 / T,
-                    ctx_sb[:, c, b, :].rearrange("p (g t) -> p g t", t=T),
-                    ALU.mult,
-                    ALU.add,
+            paragraph_sum = work.tile([P, G], F32, name="paragraph_sum")
+            nc.vector.reduce_sum(paragraph_sum[:], ctx_sb[:, c, 0, :].rearrange("p (g t) -> p g t", t=T), axis=mybir.AxisListType.X)
+            nc.vector.scalar_tensor_tensor(
+                x[0][:, cols].rearrange("p (g t) -> p g t", t=T),
+                paragraph_sum[:].unsqueeze(2).to_broadcast([P, G, T]),
+                1.0 / T,
+                ctx_sb[:, c, 0, :].rearrange("p (g t) -> p g t", t=T),
+                ALU.mult,
+                ALU.add,
+            )
+            paragraph_mean = work.tile([P, G], F32, name="paragraph_mean")
+            divided = work.tile([P, T], F32, name="divided")
+            for g in range(G):
+                nc.scalar.activation(
+                    divided[:], ctx_sb[:, c, 1, g * T : (g + 1) * T], FUNC.Copy, scale=1.0 / T, accum_out=paragraph_mean[:, g : g + 1]
+                )
+            for g in range(G):
+                first_token = c * TW + g * T
+                nc.scalar.activation(
+                    x[1][:, first_token : first_token + T], ctx_sb[:, c, 1, g * T : (g + 1) * T], FUNC.Identity, bias=paragraph_mean[:, g : g + 1]
                 )
             x_turned = turned_psum.tile([P, G, C], F32, name="x_turned")
             for g in range(G):
@@ -91,11 +104,11 @@ def tile_emencoder_kernel(tc, ctx, gain, shift, w1, b1, w2, b2, base, offs, out)
                     nc.tensor.transpose(x_turned[:, g, b * P : (b + 1) * P], x[b][:, first_token : first_token + T], identity[:])
             partial = work.tile([P, G, 6], F32, name="partial")
             mean_var = work.tile([P, G, 2], F32, name="mean_var")
+            rstd = work.tile([P, G], F32, name="rstd")
             for g in range(G):
                 nc.vector.bn_stats(partial[:, g, :], x_turned[:, g, :])
                 nc.vector.bn_aggr(mean_var[:, g, :], partial[:, g, :])
-            rstd = work.tile([P, G], F32, name="rstd")
-            nc.scalar.activation(rstd[:], mean_var[:, :, 1], FUNC.Abs_reciprocal_sqrt, bias=eps[:])
+                nc.scalar.activation(rstd[:, g : g + 1], mean_var[:, g, 1:2], FUNC.Abs_reciprocal_sqrt, bias=eps[:])
             normed_turned = work.tile([P, G, C], F32, name="normed_turned")
             for g in range(G):
                 nc.vector.tensor_scalar(

@@ -28,7 +28,7 @@ def tile_emencoder_kernel(tc, ctx, gain, shift, w1, b1, w2, b2, base, offs, out)
     with (
         tc.tile_pool(name="held", bufs=1) as held,
         tc.tile_pool(name="work", bufs=CHUNKS) as work,
-        tc.psum_pool(name="bank_psum", bufs=3) as bank_psum,
+        tc.psum_pool(name="bank_psum", bufs=4) as bank_psum,
         tc.psum_pool(name="turned_psum", bufs=2) as turned_psum,
         tc.psum_pool(name="normed_psum", bufs=1) as normed_psum,
         tc.psum_pool(name="y_psum", bufs=1) as y_psum,
@@ -139,8 +139,8 @@ def tile_emencoder_kernel(tc, ctx, gain, shift, w1, b1, w2, b2, base, offs, out)
         def project(b, first, width, y_ps):
             cols = slice(first, first + width)
             for f in range(FB):
-                nc.tensor.matmul(y_ps[:, cols], w2_sb[:, f, b * P : (b + 1) * P], h[:, f, cols], start=(f == 0), stop=(f == FB - 1))
-            nc.scalar.activation(y[b][:, cols], y_ps[:, cols], FUNC.Identity, bias=column(B2, b))
+                nc.tensor.matmul(y_ps[:], w2_sb[:, f, b * P : (b + 1) * P], h[:, f, cols], start=(f == 0), stop=(f == FB - 1))
+            nc.scalar.activation(y[b][:, cols], y_ps[:], FUNC.Identity, bias=column(B2, b))
 
         def place(b):
             nc.vector.tensor_tensor(windows[b][:].indirect(offsets[:]), y[b][:], x[b][:], ALU.add)
@@ -151,12 +151,12 @@ def tile_emencoder_kernel(tc, ctx, gain, shift, w1, b1, w2, b2, base, offs, out)
         unused_ps = bank_psum.tile([P, BANK], F32, name="unused_ps", tag="bank")
         for i in range(WARM_UP_MATMULS):
             nc.tensor.matmul(unused_ps[:], w1_sb[:, 0, 0:P], w1_sb[:, 0, 0:BANK], start=True, stop=True)
-        y_ps = y_psum.tile([P, N], F32, name="y_ps")
         for c in range(CHUNKS):
             hidden(c)
+            y_ps = y_psum.tile([P, TW], F32, name="y_ps")
             project(0, c * TW, TW, y_ps)
         place(0)
-        y_ps = y_psum.tile([P, N], F32, name="y_ps")
         for half in range(HALVES):
+            y_ps = bank_psum.tile([P, BANK], F32, name="y_ps", tag="bank")
             project(1, half * BANK, BANK, y_ps)
         place(1)

@@ -146,7 +146,8 @@ def tile_emencoder_kernel(tc, ctx, gain, shift, w1, b1, w2, b2, base, offs, out)
             nc.vector.tensor_tensor(windows[b][:].indirect(offsets[:]), y[b][:], x[b][:], ALU.add)
             nc.sync.dma_start(out[b * P : (b + 1) * P, :], windows[b][:])
 
-        for c in range(CHUNKS):
+        AHEAD = 2
+        for c in range(AHEAD):
             normalize(c)
         unused_ps = bank_psum.tile([P, BANK], F32, name="unused_ps", tag="bank")
         for i in range(WARM_UP_MATMULS):
@@ -155,6 +156,8 @@ def tile_emencoder_kernel(tc, ctx, gain, shift, w1, b1, w2, b2, base, offs, out)
             hidden(c)
             y_ps = y_psum.tile([P, TW], F32, name="y_ps")
             project(0, c * TW, TW, y_ps)
+            if c + AHEAD < CHUNKS:
+                normalize(c + AHEAD)
         place(0)
         for half in range(HALVES):
             y_ps = bank_psum.tile([P, BANK], F32, name="y_ps", tag="bank")

@@ -28,13 +28,14 @@ def tile_emencoder_kernel(tc, ctx, gain, shift, w1, b1, w2, b2, base, offs, out)
     with (
         tc.tile_pool(name="held", bufs=1) as held,
         tc.tile_pool(name="work", bufs=CHUNKS) as work,
+        tc.tile_pool(name="shared", bufs=1) as shared,
         tc.psum_pool(name="bank_psum", bufs=4) as bank_psum,
         tc.psum_pool(name="turned_psum", bufs=2) as turned_psum,
         tc.psum_pool(name="normed_psum", bufs=1) as normed_psum,
         tc.psum_pool(name="y_psum", bufs=1) as y_psum,
     ):
         ctx_blocks = ctx.rearrange("(b p) n -> p b n", p=P)
-        ctx_sb = held.tile([P, CHUNKS, CB, TW], F32, name="ctx_sb")
+        ctx_sb = shared.tile([P, CHUNKS, CB, TW], F32, name="ctx_sb", tag="shared")
         vector_rows = held.tile([P, P], F32, name="vector_rows")
         nc.gpsimd.memset(vector_rows[:], 0.0)
         for c in range(CHUNKS):
@@ -49,9 +50,6 @@ def tile_emencoder_kernel(tc, ctx, gain, shift, w1, b1, w2, b2, base, offs, out)
         nc.sync.dma_start(offsets[:], offs)
         w2_sb = held.tile([P, FB, C], BF16, name="w2_sb")
         nc.sync.dma_start(w2_sb[:], w2.rearrange("(f p) c -> p f c", p=P))
-        windows = [held.tile([P, S], F32, name=f"window{b}") for b in range(CB)]
-        for b in range(CB):
-            nc.sync.dma_start(windows[b][:], base[b * P : (b + 1) * P, :])
 
 
         identity = held.tile([P, P], F32, name="identity")
@@ -158,6 +156,10 @@ def tile_emencoder_kernel(tc, ctx, gain, shift, w1, b1, w2, b2, base, offs, out)
             project(0, c * TW, TW, y_ps)
             if c + AHEAD < CHUNKS:
                 normalize(c + AHEAD)
+            if c + AHEAD == CHUNKS - 1:
+                windows = [shared.tile([P, S], F32, name="window0", tag="shared"), held.tile([P, S], F32, name="window1")]
+                for b in range(CB):
+                    nc.sync.dma_start(windows[b][:], base[b * P : (b + 1) * P, :])
         place(0)
         for half in range(HALVES):
             y_ps = bank_psum.tile([P, BANK], F32, name="y_ps", tag="bank")

@@ -15,6 +15,7 @@ G = TW // T
 CHUNKS = N // TW
 BANK = 512
 HALVES = N // BANK
+EARLY_WARM_UP_MATMULS = 10
 WARM_UP_MATMULS = 8
 
 GAIN, SHIFT, B2, B1 = 0, CB, 2 * CB, 3 * CB
@@ -52,6 +53,11 @@ def tile_emencoder_kernel(tc, ctx, gain, shift, w1, b1, w2, b2, base, offs, out)
         nc.sync.dma_start(w2_sb[:], w2.rearrange("(f p) c -> p f c", p=P))
 
 
+        zeros = held.tile([P, BANK], BF16, name="zeros")
+        nc.vector.memset(zeros[:], 0.0)
+        early_unused_ps = bank_psum.tile([P, BANK], F32, name="early_unused_ps", tag="bank")
+        for i in range(EARLY_WARM_UP_MATMULS):
+            nc.tensor.matmul(early_unused_ps[:], zeros[:, 0:P], zeros[:], start=True, stop=True)
         identity = held.tile([P, P], F32, name="identity")
         make_identity(nc, identity[:])
         eps = held.tile([P, 1], F32, name="eps")

@@ -16,7 +16,7 @@ CHUNKS = N // TW
 BANK = 512
 HALVES = N // BANK
 EARLY_WARM_UP_MATMULS = 10
-WARM_UP_MATMULS = 8
+WARM_UP_MATMULS = 4
 
 GAIN, SHIFT, B2, B1 = 0, CB, 2 * CB, 3 * CB
 VECTOR_COLUMNS = 3 * CB + FB

@@ -13,9 +13,10 @@ FB = FF // P
 TW = 256
 G = TW // T
 CHUNKS = N // TW
+IN_FLIGHT = 2 * G
 BANK = 512
 HALVES = N // BANK
-EARLY_WARM_UP_MATMULS = 10
+EARLY_WARM_UP_MATMULS = 5
 WARM_UP_MATMULS = 4
 
 GAIN, SHIFT, B2, B1 = 0, CB, 2 * CB, 3 * CB
@@ -29,10 +30,11 @@ def tile_emencoder_kernel(tc, ctx, gain, shift, w1, b1, w2, b2, base, offs, out)
     with (
         tc.tile_pool(name="held", bufs=1) as held,
         tc.tile_pool(name="work", bufs=CHUNKS) as work,
+        tc.tile_pool(name="small", bufs=IN_FLIGHT) as small_pool,
         tc.tile_pool(name="shared", bufs=1) as shared,
-        tc.psum_pool(name="bank_psum", bufs=4) as bank_psum,
+        tc.psum_pool(name="bank_psum", bufs=3) as bank_psum,
         tc.psum_pool(name="turned_psum", bufs=2) as turned_psum,
-        tc.psum_pool(name="normed_psum", bufs=1) as normed_psum,
+        tc.psum_pool(name="normed_psum", bufs=2) as normed_psum,
         tc.psum_pool(name="y_psum", bufs=1) as y_psum,
     ):
         ctx_blocks = ctx.rearrange("(b p) n -> p b n", p=P)
@@ -78,52 +80,32 @@ def tile_emencoder_kernel(tc, ctx, gain, shift, w1, b1, w2, b2, base, offs, out)
         h = held.tile([P, FB, N], BF16, name="h")
         y = [held.tile([P, N], F32, name=f"y{b}") for b in range(CB)]
 
-        def normalize(c):
-            cols = slice(c * TW, (c + 1) * TW)
-            paragraph_sum = work.tile([P, G], F32, name="paragraph_sum")
-            nc.vector.reduce_sum(paragraph_sum[:], ctx_sb[:, c, 0, :].rearrange("p (g t) -> p g t", t=T), axis=mybir.AxisListType.X)
-            nc.vector.scalar_tensor_tensor(
-                x[0][:, cols].rearrange("p (g t) -> p g t", t=T),
-                paragraph_sum[:].unsqueeze(2).to_broadcast([P, G, T]),
-                1.0 / T,
-                ctx_sb[:, c, 0, :].rearrange("p (g t) -> p g t", t=T),
-                ALU.mult,
-                ALU.add,
-            )
-            paragraph_mean = work.tile([P, G], F32, name="paragraph_mean")
-            divided = work.tile([P, T], F32, name="divided")
-            for g in range(G):
-                nc.scalar.activation(
-                    divided[:], ctx_sb[:, c, 1, g * T : (g + 1) * T], FUNC.Copy, scale=1.0 / T, accum_out=paragraph_mean[:, g : g + 1]
-                )
-            for g in range(G):
-                first_token = c * TW + g * T
-                nc.scalar.activation(
-                    x[1][:, first_token : first_token + T], ctx_sb[:, c, 1, g * T : (g + 1) * T], FUNC.Identity, bias=paragraph_mean[:, g : g + 1]
-                )
-            x_turned = turned_psum.tile([P, G, C], F32, name="x_turned")
-            for g in range(G):
-                first_token = c * TW + g * T
-                for b in range(CB):
-                    nc.tensor.transpose(x_turned[:, g, b * P : (b + 1) * P], x[b][:, first_token : first_token + T], identity[:])
-            partial = work.tile([P, G, 6], F32, name="partial")
-            mean_var = work.tile([P, G, 2], F32, name="mean_var")
-            rstd = work.tile([P, G], F32, name="rstd")
-            for g in range(G):
-                nc.vector.bn_stats(partial[:, g, :], x_turned[:, g, :])
-                nc.vector.bn_aggr(mean_var[:, g, :], partial[:, g, :])
-                nc.scalar.activation(rstd[:, g : g + 1], mean_var[:, g, 1:2], FUNC.Abs_reciprocal_sqrt, bias=eps[:])
-            normed_turned = work.tile([P, G, C], F32, name="normed_turned")
-            for g in range(G):
-                nc.vector.tensor_scalar(
-                    normed_turned[:, g, :], x_turned[:, g, :], mean_var[:, g, 0:1], rstd[:, g : g + 1], ALU.subtract, ALU.mult
-                )
-            normed = normed_psum.tile([P, CB, TW], F32, name="normed")
+        def normalize(p):
+            c, g = p // G, p % G
+            cols = slice(p * T, (p + 1) * T)
+            in_chunk = slice(g * T, (g + 1) * T)
+            ctx_p = [ctx_sb[:, c, b, in_chunk] for b in range(CB)]
+            small = small_pool.tile([P, 11], F32, name="small")
+            mean0, mean1, partial, mean_var, rstd = small[:, 0:1], small[:, 1:2], small[:, 2:8], small[:, 8:10], small[:, 10:11]
+            divided0 = work.tile([P, T], F32, name="divided0")
+            nc.vector.tensor_scalar(divided0[:], ctx_p[0], 1.0 / T, None, ALU.mult, ALU.add, accum_out=mean0)
+            nc.vector.tensor_scalar(x[0][:, cols], ctx_p[0], mean0, None, ALU.add)
+            divided1 = work.tile([P, T], F32, name="divided1")
+            nc.scalar.activation(divided1[:], ctx_p[1], FUNC.Copy, scale=1.0 / T, accum_out=mean1)
+            nc.scalar.activation(x[1][:, cols], ctx_p[1], FUNC.Identity, bias=mean1)
+            x_turned = turned_psum.tile([P, C], F32, name="x_turned")
             for b in range(CB):
-                for g in range(G):
-                    nc.tensor.transpose(normed[:, b, g * T : (g + 1) * T], normed_turned[:, g, b * P : (b + 1) * P], identity[:])
+                nc.tensor.transpose(x_turned[:, b * P : (b + 1) * P], x[b][:, cols], identity[:])
+            nc.vector.bn_stats(partial, x_turned[:])
+            nc.vector.bn_aggr(mean_var, partial)
+            nc.scalar.activation(rstd, mean_var[:, 1:2], FUNC.Abs_reciprocal_sqrt, bias=eps[:])
+            normed_turned = work.tile([P, C], F32, name="normed_turned")
+            nc.vector.tensor_scalar(normed_turned[:], x_turned[:], mean_var[:, 0:1], rstd, ALU.subtract, ALU.mult)
+            normed = normed_psum.tile([P, CB, T], F32, name="normed")
             for b in range(CB):
-                nc.scalar.activation(z[c][:, b, :], normed[:, b, :], FUNC.Identity, bias=column(SHIFT, b), scale=column(GAIN, b))
+                nc.tensor.transpose(normed[:, b, :], normed_turned[:, b * P : (b + 1) * P], identity[:])
+            for b in range(CB):
+                nc.scalar.activation(z[c][:, b, in_chunk], normed[:, b, :], FUNC.Identity, bias=column(SHIFT, b), scale=column(GAIN, b))
 
         def hidden(c):
             cols = slice(c * TW, (c + 1) * TW)
@@ -151,17 +133,18 @@ def tile_emencoder_kernel(tc, ctx, gain, shift, w1, b1, w2, b2, base, offs, out)
             nc.sync.dma_start(out[b * P : (b + 1) * P, :], windows[b][:])
 
         AHEAD = 2
-        for c in range(AHEAD):
-            normalize(c)
+        for p in range(AHEAD * G):
+            normalize(p)
         unused_ps = bank_psum.tile([P, BANK], F32, name="unused_ps", tag="bank")
         for i in range(WARM_UP_MATMULS):
-            nc.tensor.matmul(unused_ps[:], w1_sb[:, 0, 0:P], w1_sb[:, 0, 0:BANK], start=True, stop=True)
+            nc.tensor.matmul(unused_ps[:, 0:P], x[0][:, T : 2 * T], x[0][:, T : 2 * T], start=True, stop=True)
         for c in range(CHUNKS):
             hidden(c)
             y_ps = y_psum.tile([P, TW], F32, name="y_ps")
             project(0, c * TW, TW, y_ps)
             if c + AHEAD < CHUNKS:
-                normalize(c + AHEAD)
+                for g in range(G):
+                    normalize((c + AHEAD) * G + g)
             if c + AHEAD == CHUNKS - 1:
                 windows = [shared.tile([P, S], F32, name="window0", tag="shared"), held.tile([P, S], F32, name="window1")]
                 for b in range(CB):

@@ -16,7 +16,7 @@ CHUNKS = N // TW
 IN_FLIGHT = 2 * G
 BANK = 512
 HALVES = N // BANK
-EARLY_WARM_UP_MATMULS = 5
+EARLY_WARM_UP_MATMULS = 4
 WARM_UP_MATMULS = 4
 
 GAIN, SHIFT, B2, B1 = 0, CB, 2 * CB, 3 * CB
@@ -32,10 +32,9 @@ def tile_emencoder_kernel(tc, ctx, gain, shift, w1, b1, w2, b2, base, offs, out)
         tc.tile_pool(name="work", bufs=CHUNKS) as work,
         tc.tile_pool(name="small", bufs=IN_FLIGHT) as small_pool,
         tc.tile_pool(name="shared", bufs=1) as shared,
-        tc.psum_pool(name="bank_psum", bufs=3) as bank_psum,
+        tc.psum_pool(name="bank_psum", bufs=4) as bank_psum,
         tc.psum_pool(name="turned_psum", bufs=2) as turned_psum,
         tc.psum_pool(name="normed_psum", bufs=2) as normed_psum,
-        tc.psum_pool(name="y_psum", bufs=1) as y_psum,
     ):
         ctx_blocks = ctx.rearrange("(b p) n -> p b n", p=P)
         ctx_sb = shared.tile([P, CHUNKS, CB, TW], F32, name="ctx_sb", tag="shared")
@@ -55,11 +54,11 @@ def tile_emencoder_kernel(tc, ctx, gain, shift, w1, b1, w2, b2, base, offs, out)
         nc.sync.dma_start(w2_sb[:], w2.rearrange("(f p) c -> p f c", p=P))
 
 
-        zeros = held.tile([P, BANK], BF16, name="zeros")
+        zeros = held.tile([P, P], F32, name="zeros")
         nc.vector.memset(zeros[:], 0.0)
-        early_unused_ps = bank_psum.tile([P, BANK], F32, name="early_unused_ps", tag="bank")
+        early_unused_ps = bank_psum.tile([P, P], F32, name="early_unused_ps", tag="bank")
         for i in range(EARLY_WARM_UP_MATMULS):
-            nc.tensor.matmul(early_unused_ps[:], zeros[:, 0:P], zeros[:], start=True, stop=True)
+            nc.tensor.matmul(early_unused_ps[:], zeros[:], zeros[:], start=True, stop=True)
         identity = held.tile([P, P], F32, name="identity")
         make_identity(nc, identity[:])
         eps = held.tile([P, 1], F32, name="eps")
@@ -93,7 +92,10 @@ def tile_emencoder_kernel(tc, ctx, gain, shift, w1, b1, w2, b2, base, offs, out)
             divided1 = work.tile([P, T], F32, name="divided1")
             nc.scalar.activation(divided1[:], ctx_p[1], FUNC.Copy, scale=1.0 / T, accum_out=mean1)
             nc.scalar.activation(x[1][:, cols], ctx_p[1], FUNC.Identity, bias=mean1)
-            x_turned = turned_psum.tile([P, C], F32, name="x_turned")
+            if c == 1:
+                x_turned = bank_psum.tile([P, C], F32, name="x_turned", tag="bank")
+            else:
+                x_turned = turned_psum.tile([P, C], F32, name="x_turned")
             for b in range(CB):
                 nc.tensor.transpose(x_turned[:, b * P : (b + 1) * P], x[b][:, cols], identity[:])
             nc.vector.bn_stats(partial, x_turned[:])
@@ -107,9 +109,9 @@ def tile_emencoder_kernel(tc, ctx, gain, shift, w1, b1, w2, b2, base, offs, out)
             for b in range(CB):
                 nc.scalar.activation(z[c][:, b, in_chunk], normed[:, b, :], FUNC.Identity, bias=column(SHIFT, b), scale=column(GAIN, b))
 
-        def hidden(c):
+        def hidden(c, pairs):
             cols = slice(c * TW, (c + 1) * TW)
-            for pair in range(FB // 2):
+            for pair in pairs:
                 h_ps = bank_psum.tile([P, 2, TW], F32, name="h_ps", tag="bank")
                 for i in range(2):
                     f = 2 * pair + i
@@ -138,13 +140,18 @@ def tile_emencoder_kernel(tc, ctx, gain, shift, w1, b1, w2, b2, base, offs, out)
         unused_ps = bank_psum.tile([P, BANK], F32, name="unused_ps", tag="bank")
         for i in range(WARM_UP_MATMULS):
             nc.tensor.matmul(unused_ps[:, 0:P], x[0][:, T : 2 * T], x[0][:, T : 2 * T], start=True, stop=True)
+        PAIRS = FB // 2
+        hidden(0, range(PAIRS))
         for c in range(CHUNKS):
-            hidden(c)
-            y_ps = y_psum.tile([P, TW], F32, name="y_ps")
-            project(0, c * TW, TW, y_ps)
             if c + AHEAD < CHUNKS:
                 for g in range(G):
                     normalize((c + AHEAD) * G + g)
+            if c + 1 < CHUNKS:
+                hidden(c + 1, range(1))
+            y_ps = bank_psum.tile([P, TW], F32, name="y_ps", tag="bank")
+            project(0, c * TW, TW, y_ps)
+            if c + 1 < CHUNKS:
+                hidden(c + 1, range(1, PAIRS))
             if c + AHEAD == CHUNKS - 1:
                 windows = [shared.tile([P, S], F32, name="window0", tag="shared"), held.tile([P, S], F32, name="window1")]
                 for b in range(CB):

@@ -17,7 +17,7 @@ IN_FLIGHT = 2 * G
 BANK = 512
 HALVES = N // BANK
 EARLY_WARM_UP_MATMULS = 4
-WARM_UP_MATMULS = 4
+WARM_UP_MATMULS = 2
 
 GAIN, SHIFT, B2, B1 = 0, CB, 2 * CB, 3 * CB
 VECTOR_COLUMNS = 3 * CB + FB
@@ -108,6 +108,7 @@ def tile_emencoder_kernel(tc, ctx, gain, shift, w1, b1, w2, b2, base, offs, out)
                 nc.tensor.transpose(normed[:, b, :], normed_turned[:, b * P : (b + 1) * P], identity[:])
             for b in range(CB):
                 nc.scalar.activation(z[c][:, b, in_chunk], normed[:, b, :], FUNC.Identity, bias=column(SHIFT, b), scale=column(GAIN, b))
+            return normed_turned
 
         def hidden(c, pairs):
             cols = slice(c * TW, (c + 1) * TW)
@@ -136,10 +137,13 @@ def tile_emencoder_kernel(tc, ctx, gain, shift, w1, b1, w2, b2, base, offs, out)
 
         AHEAD = 2
         for p in range(AHEAD * G):
-            normalize(p)
-        unused_ps = bank_psum.tile([P, BANK], F32, name="unused_ps", tag="bank")
-        for i in range(WARM_UP_MATMULS):
-            nc.tensor.matmul(unused_ps[:, 0:P], x[0][:, T : 2 * T], x[0][:, T : 2 * T], start=True, stop=True)
+            normed_turned = normalize(p)
+            if p == 0:
+                first_normed_turned = normed_turned
+        unused_ps = bank_psum.tile([P, P], F32, name="unused_ps", tag="bank")
+        for operand in (x[0][:, T : 2 * T], first_normed_turned[:, 0:P]):
+            for i in range(WARM_UP_MATMULS):
+                nc.tensor.matmul(unused_ps[:], operand, operand, start=True, stop=True)
         PAIRS = FB // 2
         hidden(0, range(PAIRS))
         for c in range(CHUNKS):

@@ -41,8 +41,9 @@ def tile_emencoder_kernel(tc, ctx, gain, shift, w1, b1, w2, b2, base, offs, out)
         vector_rows = held.tile([P, P], F32, name="vector_rows")
         nc.gpsimd.memset(vector_rows[:], 0.0)
         for c in range(CHUNKS):
-            nc.sync.dma_start(ctx_sb[:, c], ctx_blocks[:, :, c * TW : (c + 1) * TW])
-            if c == 0:
+            for first, width in [(g * T, T) for g in range(G)] if c == 0 else [(0, TW)]:
+                nc.sync.dma_start(ctx_sb[:, c, :, first : first + width], ctx_blocks[:, :, c * TW + first : c * TW + first + width])
+            if c == 1:
                 for first_row, vector in ((GAIN, gain), (SHIFT, shift), (B2, b2), (B1, b1)):
                     rows = vector.shape[0] // P
                     nc.sync.dma_start(vector_rows[first_row : first_row + rows, :], vector.rearrange("(r p) o -> r (p o)", p=P))
@@ -66,10 +67,7 @@ def tile_emencoder_kernel(tc, ctx, gain, shift, w1, b1, w2, b2, base, offs, out)
         unused_rstd = held.tile([P, 1], F32, name="unused_rstd")
         nc.scalar.activation(unused_rstd[:], eps[:], FUNC.Abs_reciprocal_sqrt, bias=eps[:])
 
-        vector_columns = bank_psum.tile([P, P], F32, name="vector_columns", tag="bank")
-        nc.tensor.transpose(vector_columns[:], vector_rows[:], identity[:])
         per_partition = held.tile([P, VECTOR_COLUMNS], F32, name="per_partition")
-        nc.vector.tensor_copy(per_partition[:], vector_columns[:, 0:VECTOR_COLUMNS])
 
         def column(first, block):
             return per_partition[:, first + block : first + block + 1]
@@ -79,13 +77,12 @@ def tile_emencoder_kernel(tc, ctx, gain, shift, w1, b1, w2, b2, base, offs, out)
         h = held.tile([P, FB, N], BF16, name="h")
         y = [held.tile([P, N], F32, name=f"y{b}") for b in range(CB)]
 
-        def normalize(p):
+        def turn(p):
             c, g = p // G, p % G
             cols = slice(p * T, (p + 1) * T)
-            in_chunk = slice(g * T, (g + 1) * T)
-            ctx_p = [ctx_sb[:, c, b, in_chunk] for b in range(CB)]
+            ctx_p = [ctx_sb[:, c, b, g * T : (g + 1) * T] for b in range(CB)]
             small = small_pool.tile([P, 11], F32, name="small")
-            mean0, mean1, partial, mean_var, rstd = small[:, 0:1], small[:, 1:2], small[:, 2:8], small[:, 8:10], small[:, 10:11]
+            mean0, mean1 = small[:, 0:1], small[:, 1:2]
             divided0 = work.tile([P, T], F32, name="divided0")
             nc.vector.tensor_scalar(divided0[:], ctx_p[0], 1.0 / T, None, ALU.mult, ALU.add, accum_out=mean0)
             nc.vector.tensor_scalar(x[0][:, cols], ctx_p[0], mean0, None, ALU.add)
@@ -98,6 +95,11 @@ def tile_emencoder_kernel(tc, ctx, gain, shift, w1, b1, w2, b2, base, offs, out)
                 x_turned = turned_psum.tile([P, C], F32, name="x_turned")
             for b in range(CB):
                 nc.tensor.transpose(x_turned[:, b * P : (b + 1) * P], x[b][:, cols], identity[:])
+            return small, x_turned
+
+        def normalize(p, small, x_turned):
+            c, g = p // G, p % G
+            partial, mean_var, rstd = small[:, 2:8], small[:, 8:10], small[:, 10:11]
             nc.vector.bn_stats(partial, x_turned[:])
             nc.vector.bn_aggr(mean_var, partial)
             nc.scalar.activation(rstd, mean_var[:, 1:2], FUNC.Abs_reciprocal_sqrt, bias=eps[:])
@@ -107,7 +109,9 @@ def tile_emencoder_kernel(tc, ctx, gain, shift, w1, b1, w2, b2, base, offs, out)
             for b in range(CB):
                 nc.tensor.transpose(normed[:, b, :], normed_turned[:, b * P : (b + 1) * P], identity[:])
             for b in range(CB):
-                nc.scalar.activation(z[c][:, b, in_chunk], normed[:, b, :], FUNC.Identity, bias=column(SHIFT, b), scale=column(GAIN, b))
+                nc.scalar.activation(
+                    z[c][:, b, g * T : (g + 1) * T], normed[:, b, :], FUNC.Identity, bias=column(SHIFT, b), scale=column(GAIN, b)
+                )
             return normed_turned
 
         def hidden(c, pairs):
@@ -136,12 +140,13 @@ def tile_emencoder_kernel(tc, ctx, gain, shift, w1, b1, w2, b2, base, offs, out)
             nc.sync.dma_start(out[b * P : (b + 1) * P, :], windows[b][:])
 
         AHEAD = 2
-        for p in range(AHEAD * G):
-            normed_turned = normalize(p)
-            if p == 0:
-                first_normed_turned = normed_turned
+        turned = [turn(p) for p in range(AHEAD * G)]
+        vector_columns = bank_psum.tile([P, P], F32, name="vector_columns", tag="bank")
+        nc.tensor.transpose(vector_columns[:], vector_rows[:], identity[:])
+        nc.vector.tensor_copy(per_partition[:], vector_columns[:, 0:VECTOR_COLUMNS])
+        normed_turned = [normalize(p, *turned[p]) for p in range(AHEAD * G)]
         unused_ps = bank_psum.tile([P, P], F32, name="unused_ps", tag="bank")
-        for operand in (x[0][:, T : 2 * T], first_normed_turned[:, 0:P]):
+        for operand in (x[0][:, T : 2 * T], normed_turned[0][:, 0:P]):
             for i in range(WARM_UP_MATMULS):
                 nc.tensor.matmul(unused_ps[:], operand, operand, start=True, stop=True)
         PAIRS = FB // 2
@@ -149,7 +154,8 @@ def tile_emencoder_kernel(tc, ctx, gain, shift, w1, b1, w2, b2, base, offs, out)
         for c in range(CHUNKS):
             if c + AHEAD < CHUNKS:
                 for g in range(G):
-                    normalize((c + AHEAD) * G + g)
+                    p = (c + AHEAD) * G + g
+                    normalize(p, *turn(p))
             if c + 1 < CHUNKS:
                 hidden(c + 1, range(1))
             y_ps = bank_psum.tile([P, TW], F32, name="y_ps", tag="bank")

@@ -133,7 +133,10 @@ def tile_emencoder_kernel(tc, ctx, gain, shift, w1, b1, w2, b2, base, offs, out)
             cols = slice(first, first + width)
             for f in range(FB):
                 nc.tensor.matmul(y_ps[:], w2_sb[:, f, b * P : (b + 1) * P], h[:, f, cols], start=(f == 0), stop=(f == FB - 1))
-            nc.scalar.activation(y[b][:, cols], y_ps[:], FUNC.Identity, bias=column(B2, b))
+            if b == 0 and first + width == N:
+                nc.vector.tensor_scalar(y[b][:, cols], y_ps[:], column(B2, b), None, ALU.add)
+            else:
+                nc.scalar.activation(y[b][:, cols], y_ps[:], FUNC.Identity, bias=column(B2, b))
 
         def place(b):
             nc.vector.tensor_tensor(windows[b][:].indirect(offsets[:]), y[b][:], x[b][:], ALU.add)

import concourse.mybir as mybir
from concourse.masks import make_identity

F32, BF16, U16 = mybir.dt.float32, mybir.dt.bfloat16, mybir.dt.uint16
ALU = mybir.AluOpType
FUNC = mybir.ActivationFunctionType

P = 128
C, FF, S, N, T = 256, 1024, 2048, 1024, 128
EPS = 1e-6
CB = C // P
FB = FF // P
TW = 256
G = TW // T
CHUNKS = N // TW
IN_FLIGHT = 2 * G
BANK = 512
HALVES = N // BANK
EARLY_WARM_UP_MATMULS = 4
WARM_UP_MATMULS = 2

GAIN, SHIFT, B2, B1 = 0, CB, 2 * CB, 3 * CB
VECTOR_COLUMNS = 3 * CB + FB

FLOPS = 2 * C * FF * N * 2


def tile_emencoder_kernel(tc, ctx, gain, shift, w1, b1, w2, b2, base, offs, out):
    nc = tc.nc
    with (
        tc.tile_pool(name="held", bufs=1) as held,
        tc.tile_pool(name="work", bufs=CHUNKS) as work,
        tc.tile_pool(name="small", bufs=IN_FLIGHT) as small_pool,
        tc.tile_pool(name="shared", bufs=1) as shared,
        tc.psum_pool(name="bank_psum", bufs=4) as bank_psum,
        tc.psum_pool(name="turned_psum", bufs=2) as turned_psum,
        tc.psum_pool(name="normed_psum", bufs=2) as normed_psum,
    ):
        ctx_blocks = ctx.rearrange("(b p) n -> p b n", p=P)
        ctx_sb = shared.tile([P, CHUNKS, CB, TW], F32, name="ctx_sb", tag="shared")
        vector_rows = held.tile([P, P], F32, name="vector_rows")
        nc.gpsimd.memset(vector_rows[:], 0.0)
        for c in range(CHUNKS):
            for first, width in [(g * T, T) for g in range(G)] if c == 0 else [(0, TW)]:
                nc.sync.dma_start(ctx_sb[:, c, :, first : first + width], ctx_blocks[:, :, c * TW + first : c * TW + first + width])
            if c == 1:
                for first_row, vector in ((GAIN, gain), (SHIFT, shift), (B2, b2), (B1, b1)):
                    rows = vector.shape[0] // P
                    nc.sync.dma_start(vector_rows[first_row : first_row + rows, :], vector.rearrange("(r p) o -> r (p o)", p=P))
        w1_sb = held.tile([P, CB, FF], BF16, name="w1_sb")
        nc.sync.dma_start(w1_sb[:], w1.rearrange("(k p) f -> p k f", p=P))
        offsets = held.tile([P, N // 16], U16, name="offsets")
        nc.sync.dma_start(offsets[:], offs)
        w2_sb = held.tile([P, FB, C], BF16, name="w2_sb")
        nc.sync.dma_start(w2_sb[:], w2.rearrange("(f p) c -> p f c", p=P))


        zeros = held.tile([P, P], F32, name="zeros")
        nc.vector.memset(zeros[:], 0.0)
        early_unused_ps = bank_psum.tile([P, P], F32, name="early_unused_ps", tag="bank")
        for i in range(EARLY_WARM_UP_MATMULS):
            nc.tensor.matmul(early_unused_ps[:], zeros[:], zeros[:], start=True, stop=True)
        identity = held.tile([P, P], F32, name="identity")
        make_identity(nc, identity[:])
        eps = held.tile([P, 1], F32, name="eps")
        nc.vector.memset(eps[:], EPS)
        unused_rstd = held.tile([P, 1], F32, name="unused_rstd")
        nc.scalar.activation(unused_rstd[:], eps[:], FUNC.Abs_reciprocal_sqrt, bias=eps[:])

        per_partition = held.tile([P, VECTOR_COLUMNS], F32, name="per_partition")

        def column(first, block):
            return per_partition[:, first + block : first + block + 1]

        x = [held.tile([P, N], F32, name=f"x{b}") for b in range(CB)]
        z = [held.tile([P, CB, TW], BF16, name=f"z{c}") for c in range(CHUNKS)]
        h = held.tile([P, FB, N], BF16, name="h")
        y = [held.tile([P, N], F32, name=f"y{b}") for b in range(CB)]

        def turn(p):
            c, g = p // G, p % G
            cols = slice(p * T, (p + 1) * T)
            ctx_p = [ctx_sb[:, c, b, g * T : (g + 1) * T] for b in range(CB)]
            small = small_pool.tile([P, 11], F32, name="small")
            mean0, mean1 = small[:, 0:1], small[:, 1:2]
            divided0 = work.tile([P, T], F32, name="divided0")
            nc.vector.tensor_scalar(divided0[:], ctx_p[0], 1.0 / T, None, ALU.mult, ALU.add, accum_out=mean0)
            nc.vector.tensor_scalar(x[0][:, cols], ctx_p[0], mean0, None, ALU.add)
            divided1 = work.tile([P, T], F32, name="divided1")
            nc.scalar.activation(divided1[:], ctx_p[1], FUNC.Copy, scale=1.0 / T, accum_out=mean1)
            nc.scalar.activation(x[1][:, cols], ctx_p[1], FUNC.Identity, bias=mean1)
            if c == 1:
                x_turned = bank_psum.tile([P, C], F32, name="x_turned", tag="bank")
            else:
                x_turned = turned_psum.tile([P, C], F32, name="x_turned")
            for b in range(CB):
                nc.tensor.transpose(x_turned[:, b * P : (b + 1) * P], x[b][:, cols], identity[:])
            return small, x_turned

        def normalize(p, small, x_turned):
            c, g = p // G, p % G
            partial, mean_var, rstd = small[:, 2:8], small[:, 8:10], small[:, 10:11]
            nc.vector.bn_stats(partial, x_turned[:])
            nc.vector.bn_aggr(mean_var, partial)
            nc.scalar.activation(rstd, mean_var[:, 1:2], FUNC.Abs_reciprocal_sqrt, bias=eps[:])
            normed_turned = work.tile([P, C], F32, name="normed_turned")
            nc.vector.tensor_scalar(normed_turned[:], x_turned[:], mean_var[:, 0:1], rstd, ALU.subtract, ALU.mult)
            normed = normed_psum.tile([P, CB, T], F32, name="normed")
            for b in range(CB):
                nc.tensor.transpose(normed[:, b, :], normed_turned[:, b * P : (b + 1) * P], identity[:])
            for b in range(CB):
                nc.scalar.activation(
                    z[c][:, b, g * T : (g + 1) * T], normed[:, b, :], FUNC.Identity, bias=column(SHIFT, b), scale=column(GAIN, b)
                )
            return normed_turned

        def hidden(c, pairs):
            cols = slice(c * TW, (c + 1) * TW)
            for pair in pairs:
                h_ps = bank_psum.tile([P, 2, TW], F32, name="h_ps", tag="bank")
                for i in range(2):
                    f = 2 * pair + i
                    for k in range(CB):
                        nc.tensor.matmul(h_ps[:, i, :], w1_sb[:, k, f * P : (f + 1) * P], z[c][:, k, :], start=(k == 0), stop=(k == CB - 1))
                for i in range(2):
                    f = 2 * pair + i
                    if pair % 4 == 3:
                        nc.vector.tensor_scalar(h[:, f, cols], h_ps[:, i, :], column(B1, f), 0.0, ALU.add, ALU.max)
                    else:
                        nc.scalar.activation(h[:, f, cols], h_ps[:, i, :], FUNC.Relu, bias=column(B1, f))

        def project(b, first, width, y_ps):
            cols = slice(first, first + width)
            for f in range(FB):
                nc.tensor.matmul(y_ps[:], w2_sb[:, f, b * P : (b + 1) * P], h[:, f, cols], start=(f == 0), stop=(f == FB - 1))
            if b == 0 and first + width == N:
                nc.vector.tensor_scalar(y[b][:, cols], y_ps[:], column(B2, b), None, ALU.add)
            else:
                nc.scalar.activation(y[b][:, cols], y_ps[:], FUNC.Identity, bias=column(B2, b))

        def place(b):
            nc.vector.tensor_tensor(windows[b][:].indirect(offsets[:]), y[b][:], x[b][:], ALU.add)
            nc.sync.dma_start(out[b * P : (b + 1) * P, :], windows[b][:])

        AHEAD = 2
        turned = [turn(p) for p in range(AHEAD * G)]
        vector_columns = bank_psum.tile([P, P], F32, name="vector_columns", tag="bank")
        nc.tensor.transpose(vector_columns[:], vector_rows[:], identity[:])
        nc.vector.tensor_copy(per_partition[:], vector_columns[:, 0:VECTOR_COLUMNS])
        normed_turned = [normalize(p, *turned[p]) for p in range(AHEAD * G)]
        unused_ps = bank_psum.tile([P, P], F32, name="unused_ps", tag="bank")
        for operand in (x[0][:, T : 2 * T], normed_turned[0][:, 0:P]):
            for i in range(WARM_UP_MATMULS):
                nc.tensor.matmul(unused_ps[:], operand, operand, start=True, stop=True)
        PAIRS = FB // 2
        hidden(0, range(PAIRS))
        for c in range(CHUNKS):
            if c + AHEAD < CHUNKS:
                for g in range(G):
                    p = (c + AHEAD) * G + g
                    normalize(p, *turn(p))
            if c + 1 < CHUNKS:
                hidden(c + 1, range(1))
            y_ps = bank_psum.tile([P, TW], F32, name="y_ps", tag="bank")
            project(0, c * TW, TW, y_ps)
            if c + 1 < CHUNKS:
                hidden(c + 1, range(1, PAIRS))
            if c + AHEAD == CHUNKS - 1:
                windows = [shared.tile([P, S], F32, name="window0", tag="shared"), held.tile([P, S], F32, name="window1")]
                for b in range(CB):
                    nc.sync.dma_start(windows[b][:], base[b * P : (b + 1) * P, :])
        place(0)
        for half in range(HALVES):
            y_ps = bank_psum.tile([P, BANK], F32, name="y_ps", tag="bank")
            project(1, half * BANK, BANK, y_ps)
        place(1)
